import numpy as np
import ml_dtypes


def mxq(x, axis, fmt="e4m3"):
    dtype, down = {"e4m3": (ml_dtypes.float8_e4m3fn, 7), "e5m2": (ml_dtypes.float8_e5m2, 14)}[fmt]
    v = np.moveaxis(np.asarray(x, np.float32).astype(ml_dtypes.bfloat16).astype(np.float64), axis, -1)
    blocks = v.reshape(v.shape[:-1] + (-1, 32))
    amax = np.abs(blocks).max(-1, keepdims=True)
    byte = np.maximum(np.where(amax > 0, np.frexp(amax)[1] - 1 + 127, 0) - down, 1)
    scale = np.exp2(byte - 127.0)
    codes = (blocks / scale).astype(np.float32).astype(dtype).astype(np.float64)
    return np.moveaxis((codes * scale).reshape(v.shape), -1, axis)


WIDE = False


def mx_kscale(k):
    if not WIDE:
        return np.ones(k)
    levels = np.array([10, -10, 5, -5, 0])
    if k % 512:
        return np.exp2(np.random.permutation(np.resize(levels, k // 32))).repeat(32)
    a = np.empty((k // 512, 16))
    for p in range(k // 512):
        a[p, :8] = np.random.permutation(np.resize(levels, 8))
        for g in range(8):
            far = levels[np.abs(levels - a[p, g]) >= 10]
            a[p, g + 8] = far[np.random.randint(len(far))]
    return np.exp2(a.ravel()).repeat(32)


BF16 = ml_dtypes.bfloat16


def bf(x):
    return np.asarray(x, np.float32).astype(BF16)


def f64(x):
    return np.asarray(x).astype(np.float64)


B, N, SIZE, CH = 256, 16, 1024, 512


def sigmoid(v):
    return 1.0 / (1.0 + np.exp(-v))


def setup_inputs():
    s = mx_kscale(SIZE)
    half = np.concatenate([np.ones(CH), np.full(CH, 2.0 / np.sqrt(N))])
    return {"z_node": bf(np.random.standard_normal((B, N, SIZE)) * s),
            "z_children": bf(np.random.standard_normal((B, N, SIZE)) * half),
            "W_f": bf(np.random.standard_normal((CH, SIZE)) / np.sqrt(SIZE) / s),
            "U_f": bf(np.random.standard_normal((CH, CH)) / np.sqrt(CH)),
            "b_f": bf(np.random.standard_normal(CH) * 0.5)}


def core(z_node, z_children, W_f, U_f, b_f):
    h_k = f64(z_children)[..., :CH]
    c_k = f64(z_children)[..., CH:]
    f_j_k = sigmoid((mxq(f64(z_node), 2, "e4m3") @ mxq(f64(W_f), 1, "e4m3").T) + h_k @ f64(U_f).T + f64(b_f))
    return (f_j_k * c_k).sum(axis=1)


def e4m3fn_bytes(y):
    return np.clip(np.asarray(y, np.float64), -448.0, 448.0).astype(np.float32).astype(ml_dtypes.float8_e4m3fn).view(np.uint8)


def reference(z_node, z_children, W_f, U_f, b_f):
    out = core(z_node, z_children, W_f, U_f, b_f)
    s = np.max(np.abs(out)) / 448.0
    return out, e4m3fn_bytes(out / s)

@@ -1,0 +1,317 @@
+from contextlib import ExitStack
+
+import concourse.mybir as mybir
+from concourse.masks import make_identity
+
+F32 = mybir.dt.float32
+BF16 = mybir.dt.bfloat16
+U32 = mybir.dt.uint32
+U8 = mybir.dt.uint8
+FP8X4 = mybir.dt.float8_e4m3fn_x4
+FP8 = mybir.dt.float8_e4m3fn
+ALU = mybir.AluOpType
+ACT = mybir.ActivationFunctionType
+AX = mybir.AxisListType
+
+P = 128
+NODES, KIDS, SIZE, CH = 256, 16, 1024, 512
+FLOPS = 2 * NODES * KIDS * CH * (SIZE + CH)
+STEPS = 16
+STEPS_PER_HALF = 8
+LAST = STEPS - 1
+G_COLS = 384
+
+
+def tile_treelstm_pa_kernel(tc, z_node, z_children, W_f, U_f, b_f, out_0, out_1):
+    nc = tc.nc
+    zn = z_node.rearrange("(h p) n k -> h p n k", p=P)
+    zc = z_children.rearrange("(h p) n k -> h p n k", p=P)
+
+    with ExitStack() as ctx:
+        keep = ctx.enter_context(tc.tile_pool(name="keep", bufs=1))
+        work = ctx.enter_context(tc.tile_pool(name="work", bufs=2))
+        psum = ctx.enter_context(tc.psum_pool(name="psum", bufs=2))
+        ctx.enter_context(tc.manual_schedule())
+
+        def bank(tag, bufs):
+            return psum.tile([P, 512], F32, name=tag, bufs=bufs)
+
+        def run(calls):
+            for call in calls:
+                call()
+
+        ident = keep.tile([P, P], F32, name="ident")
+        make_identity(nc, ident[:])
+        brow = keep.tile([P, CH], BF16, name="brow")
+        nc.gpsimd.memset(brow[:], 0.0)
+        nc.gpsimd.dma_start(out=brow[0:1, :], in_=b_f.rearrange("(o c) -> o c", o=1))
+        ones = keep.tile([P, P], BF16, name="ones")
+        nc.gpsimd.memset(ones[:], 1.0)
+        zcol = keep.tile([P, 1], F32, name="zcol")
+        nc.vector.memset(zcol[:], 0.0)
+        warm = keep.tile([P, 1], F32, name="warm")
+        nc.scalar.activation(out=warm[:], in_=zcol[:], func=ACT.Sigmoid)
+
+        u_raw = keep.tile([P, 4, CH], BF16, name="u_raw")
+        nc.sync.dma_start(out=u_raw[:], in_=U_f.rearrange("(t p) k -> p t k", p=P))
+        kid = []
+        node = []
+        for j in range(STEPS):
+            kid.append(keep.tile([P, 2, SIZE], BF16, name="kid%d" % j))
+            node.append(keep.tile([P, 2, SIZE], BF16, name="node%d" % j))
+
+        def load(dst, src, j):
+            h, jj = divmod(j, STEPS_PER_HALF)
+            nc.sync.dma_start(out=dst[j][:], in_=src[h, :, 2 * jj : 2 * jj + 2, :])
+
+        load(kid, zc, 0)
+        w_raw = []
+        for t in range(4):
+            w_raw.append(keep.tile([P, SIZE], BF16, name="w_raw%d" % t))
+            nc.sync.dma_start(out=w_raw[t][:], in_=W_f[t * P : (t + 1) * P, :])
+        load(node, zn, 0)
+        for j in range(1, STEPS):
+            load(node, zn, j)
+            load(kid, zc, j)
+
+        def turn(dst, q, src):
+            return lambda: nc.tensor.transpose(out=dst[:, q * P : (q + 1) * P], in_=src, identity=ident[:])
+
+        def turn_every_2nd_word(dst, words):
+            return [turn(dst, 2 * g + u, words[:, 256 * g + u : 256 * (g + 1) : 2]) for g in range(2) for u in range(2)]
+
+        def interleaved(src):
+            return src[:].rearrange("p (g u r) -> p g r u", g=2, u=2)
+
+        u_words = u_raw[:].bitcast(F32)
+        ut = keep.tile([P, 4, CH], BF16, name="ut")
+        for u in range(2):
+            ps = bank("pl", 2)
+            run([turn(ps, t, u_words[:, t, P * u : P * (u + 1)]) for t in range(4)])
+            src = ps[:].bitcast(BF16).rearrange("p (c e) -> p e c", e=2)
+            if u == 0:
+                nc.vector.tensor_copy(out=ut[:, 0:2, :], in_=src)
+            else:
+                nc.scalar.copy(out=ut[:, 2:4, :], in_=src)
+
+        zp, ht_ps, zt_ps, ht_sb, grouped, codes, scl = {}, {}, {}, {}, {}, {}, {}
+        pl_ps, mx_ps, tmp, s_sb, f_sb, p_sb = {}, {}, {}, {}, {}, {}
+        acc = [keep.tile([P, 2, CH], F32, name="acc%d" % h) for h in range(2)]
+
+        def permute(j):
+            zp[j] = work.tile([P, 2 * SIZE], BF16, name="zp")
+            nc.scalar.copy(
+                out=zp[j][:].bitcast(F32).rearrange("p (q u i) -> p q u i", q=4, u=2),
+                in_=node[j][:].rearrange("p a k -> p (a k)").bitcast(F32).rearrange("p (q i u) -> p q u i", q=4, u=2),
+            )
+
+        def transposes(j):
+            ht_ps[j] = bank("ht", 1)
+            kw = kid[j][:].bitcast(F32)
+            calls = [turn(ht_ps[j], 2 * a + u, kw[:, a, P * u : P * (u + 1)]) for a in range(2) for u in range(2)]
+            for a in range(2):
+                zt_ps[j, a] = bank("zt", 2)
+                if j in zp:
+                    words = zp[j][:].bitcast(F32)
+                    calls.extend([turn(zt_ps[j, a], q, words[:, (4 * a + q) * P : (4 * a + q + 1) * P]) for q in range(4)])
+                else:
+                    calls.extend(turn_every_2nd_word(zt_ps[j, a], node[j][:].bitcast(F32)[:, a, :]))
+            return calls
+
+        def evacuate_h(j):
+            ht_sb[j] = work.tile([P, 2 * CH], BF16, name="ht_sb")
+            nc.scalar.copy(out=ht_sb[j][:].bitcast(F32), in_=ht_ps[j][:])
+
+        def evacuate_z(j):
+            grouped[j] = work.tile([P, 2, SIZE], BF16, name="grouped", align_bytes=64)
+            for a in range(2):
+                nc.scalar.copy(
+                    out=grouped[j][:, a, :].bitcast(F32).rearrange("p (g r u) -> p g r u", g=2, u=2),
+                    in_=interleaved(zt_ps[j, a]),
+                )
+
+        def quantize(j):
+            codes[j] = work.tile([P, 4 * P], U32, name="codes", align_bytes=64)
+            scl[j] = work.tile([P, 4 * P], U8, name="scl", align_bytes=64)
+            nc.vector.quantize_mx(
+                out=codes[j][:].bitcast(FP8X4), scales=scl[j][:], in_=grouped[j][:].rearrange("p a k -> p (a k)")
+            )
+
+        def plain(j, a, with_bias=False):
+            pl_ps[j, a] = bank("pl", 2)
+            dst = pl_ps[j, a]
+            calls = []
+            if with_bias:
+                calls.append(lambda: nc.tensor.matmul(out=dst[:], lhsT=ones[:], rhs=brow[:], start=True, stop=False))
+            for q in range(4):
+                u, e = divmod(q, 2)
+                base = (2 * a + u) * 256
+                calls.append(
+                    lambda q=q, base=base, e=e: nc.tensor.matmul(
+                        out=dst[:],
+                        lhsT=ht_sb[j][:, base + e : base + 256 : 2],
+                        rhs=ut[:, q, :],
+                        start=(q == 0 and not with_bias),
+                        stop=(q == 3),
+                    )
+                )
+            return calls
+
+        def mx(j, a):
+            mx_ps[j, a] = bank("mx", 2)
+            for g in range(2):
+                cols = slice((2 * a + g) * P, (2 * a + g + 1) * P)
+                wcols = slice(g * CH, (g + 1) * CH)
+                nc.tensor.matmul_mx(
+                    out=mx_ps[j, a][:],
+                    lhsT=codes[j][:, cols].bitcast(FP8X4),
+                    lhsT_scale=scl[j][:, cols],
+                    rhs=wcodes[:, wcols].bitcast(FP8X4),
+                    rhs_scale=wscl[:, wcols],
+                    start=(g == 0),
+                    stop=(g == 1),
+                )
+
+        def add_bias(j, a):
+            tmp[j, a] = work.tile([P, CH], F32, name="tmp")
+            nc.vector.tensor_tensor(out=tmp[j, a][:], in0=pl_ps[j, a][:], in1=bias_sb[:], op=ALU.add)
+
+        def empty_plain(j, a):
+            tmp[j, a] = work.tile([P, CH], F32, name="tmp")
+            nc.scalar.copy(out=tmp[j, a][:], in_=pl_ps[j, a][:])
+
+        def add_mx(j, a):
+            s_sb[j, a] = work.tile([P, CH], F32, name="s%d" % a)
+            nc.vector.tensor_tensor(out=s_sb[j, a][:], in0=mx_ps[j, a][:], in1=tmp[j, a][:], op=ALU.add)
+
+        def gate(j, a):
+            f_sb[j, a] = work.tile([P, CH], F32, name="f%d" % a)
+            nc.scalar.activation(out=f_sb[j, a][:], in_=s_sb[j, a][:], func=ACT.Sigmoid)
+
+        def times_cell(j, a):
+            h, jj = divmod(j, STEPS_PER_HALF)
+            if jj == 0:
+                dst = acc[h]
+            else:
+                if a == 0:
+                    p_sb[j] = work.tile([P, 2, CH], F32, name="prod")
+                dst = p_sb[j]
+            nc.vector.tensor_tensor(out=dst[:, a, :], in0=f_sb[j, a][:], in1=kid[j][:, a, CH:SIZE], op=ALU.mult)
+
+        def accumulate(j, engine, cols):
+            h, jj = divmod(j, STEPS_PER_HALF)
+            if jj > 0:
+                engine.tensor_tensor(out=acc[h][:, :, cols], in0=acc[h][:, :, cols], in1=p_sb[j][:, :, cols], op=ALU.add)
+
+        o_sb = [keep.tile([P, CH], F32, name="o%d" % h) for h in range(2)]
+        part = keep.tile([P, 2], F32, name="part")
+
+        def store_and_reduce(h):
+            nc.sync.dma_start(out=out_0[h * P : (h + 1) * P, :], in_=o_sb[h][:])
+            nc.vector.tensor_reduce(
+                out=part[:, h : h + 1], in_=o_sb[h][:], axis=AX.X, op=ALU.max, apply_absolute_value=True
+            )
+
+        def spread_part(h):
+            nc.tensor.transpose(
+                out=spread[:, h * P : (h + 1) * P], in_=part[:, h : h + 1].to_broadcast([P, P]), identity=ident[:]
+            )
+
+        wgrouped = keep.tile([P, 2, 4 * CH], BF16, name="wgrouped", align_bytes=64)
+        wg_words = wgrouped[:].bitcast(F32).rearrange("p g (c u) -> p g c u", u=2)
+        wcodes = keep.tile([P, 2 * CH], U32, name="wcodes", align_bytes=64)
+        wscl = keep.tile([P, 2 * CH], U8, name="wscl", align_bytes=64)
+
+        def turn_w(t):
+            ps = bank("mx", 2)
+            run(turn_every_2nd_word(ps, w_raw[t][:].bitcast(F32)))
+            dst = wg_words[:, :, t * P : (t + 1) * P, :]
+            if t % 2 == 0:
+                nc.vector.tensor_copy(out=dst, in_=interleaved(ps))
+            else:
+                nc.scalar.copy(out=dst, in_=interleaved(ps))
+
+        first = transposes(0)
+        run(first[0:4])
+        for t in range(4):
+            turn_w(t)
+        run(first[4:12])
+        bias_ps = bank("aux", 1)
+        nc.tensor.matmul(out=bias_ps[:], lhsT=ones[:], rhs=brow[:], start=True, stop=True)
+        bias_sb = keep.tile([P, CH], F32, name="bias_sb")
+        nc.vector.tensor_copy(out=bias_sb[:], in_=bias_ps[:])
+        evacuate_h(0)
+        evacuate_z(0)
+        permute(1)
+        for g in range(2):
+            wcols = slice(g * CH, (g + 1) * CH)
+            nc.vector.quantize_mx(out=wcodes[:, wcols].bitcast(FP8X4), scales=wscl[:, wcols], in_=wgrouped[:, g, :])
+        quantize(0)
+
+        spread = bank("aux", 1)
+        for j in range(LAST):
+            if j == STEPS_PER_HALF + 2:
+                spread_part(0)
+            turns = transposes(j + 1)
+            pa = plain(j, 0)
+            pb = plain(j, 1)
+            run(pa + turns[0:6] + pb[0:2] + turns[6:12] + pb[2:4])
+            mx(j, 0)
+            mx(j, 1)
+            evacuate_h(j + 1)
+            evacuate_z(j + 1)
+            if j + 2 <= LAST:
+                permute(j + 2)
+            add_bias(j, 0)
+            add_bias(j, 1)
+            add_mx(j, 0)
+            add_mx(j, 1)
+            gate(j, 0)
+            gate(j, 1)
+            if j >= 1:
+                accumulate(j - 1, nc.gpsimd, slice(0, G_COLS))
+            quantize(j + 1)
+            if j >= 1:
+                accumulate(j - 1, nc.vector, slice(G_COLS, CH))
+            times_cell(j, 0)
+            times_cell(j, 1)
+            if j == STEPS_PER_HALF:
+                nc.vector.tensor_tensor(out=o_sb[0][:], in0=acc[0][:, 0, :], in1=acc[0][:, 1, :], op=ALU.add)
+                store_and_reduce(0)
+
+        run(plain(LAST, 0, with_bias=True))
+        mx(LAST, 0)
+        run(plain(LAST, 1, with_bias=True))
+        mx(LAST, 1)
+        accumulate(LAST - 1, nc.gpsimd, slice(0, G_COLS))
+        accumulate(LAST - 1, nc.vector, slice(G_COLS, CH))
+        empty_plain(LAST, 0)
+        add_mx(LAST, 0)
+        gate(LAST, 0)
+        empty_plain(LAST, 1)
+        times_cell(LAST, 0)
+        add_mx(LAST, 1)
+        gate(LAST, 1)
+        nc.vector.tensor_tensor(out=o_sb[1][:], in0=acc[1][:, 0, :], in1=acc[1][:, 1, :], op=ALU.add)
+        nc.vector.tensor_tensor(out=o_sb[1][:], in0=o_sb[1][:], in1=p_sb[LAST][:, 0, :], op=ALU.add)
+        times_cell(LAST, 1)
+        nc.vector.tensor_tensor(out=o_sb[1][:], in0=o_sb[1][:], in1=p_sb[LAST][:, 1, :], op=ALU.add)
+        store_and_reduce(1)
+        spread_part(1)
+
+        junk = keep.tile([P, 2 * P], F32, name="junk")
+        scale = keep.tile([P, 1], F32, name="scale")
+        nc.vector.tensor_scalar(
+            out=junk[:], in0=spread[:, 0 : 2 * P], scalar1=1.0 / 448.0, scalar2=None, op0=ALU.mult, op1=ALU.max,
+            accum_out=scale[:, 0:1],
+        )
+        factor = keep.tile([P, 1], F32, name="factor")
+        nc.vector.reciprocal(out=factor[:], in_=scale[:])
+        o8 = keep.tile([P, 2, CH], FP8, name="o8")
+        nc.vector.tensor_scalar(
+            out=o8[:, 1, :], in0=o_sb[1][:], scalar1=factor[:, 0:1], scalar2=None, op0=ALU.mult, saturate=False
+        )
+        nc.scalar.activation(
+            out=o8[:, 0, :], in_=o_sb[0][:], func=ACT.Identity, scale=factor[:, 0:1], bias=zcol[:, 0:1], saturate=False
+        )
+        nc.sync.dma_start(out=out_1.rearrange("(h p) c -> p h c", p=P), in_=o8[:].bitcast(U8))

@@ -19,7 +19,13 @@ FLOPS = 2 * NODES * KIDS * CH * (SIZE + CH)
 STEPS = 16
 STEPS_PER_HALF = 8
 LAST = STEPS - 1
+HALF = CH // 2
 G_COLS = 384
+WARM = 6
+SPLIT = 2
+BIASED = (LAST,)
+WEAVE = (2, 2, 2, 2, 2, 1, 1, 0)
+TAIL_G_COLS = 128
 
 
 def tile_treelstm_pa_kernel(tc, z_node, z_children, W_f, U_f, b_f, out_0, out_1):
@@ -40,13 +46,15 @@ def tile_treelstm_pa_kernel(tc, z_node, z_children, W_f, U_f, b_f, out_0, out_1)
             for call in calls:
                 call()
 
-        ident = keep.tile([P, P], F32, name="ident")
-        make_identity(nc, ident[:])
-        brow = keep.tile([P, CH], BF16, name="brow")
-        nc.gpsimd.memset(brow[:], 0.0)
-        nc.gpsimd.dma_start(out=brow[0:1, :], in_=b_f.rearrange("(o c) -> o c", o=1))
         ones = keep.tile([P, P], BF16, name="ones")
         nc.gpsimd.memset(ones[:], 1.0)
+        zeros = keep.tile([P, CH], BF16, name="zeros")
+        nc.vector.memset(zeros[:], 0.0)
+        brow = keep.tile([P, CH], BF16, name="brow")
+        nc.vector.memset(brow[:], 0.0)
+        nc.scalar.dma_start(out=brow[0:1, :], in_=b_f.rearrange("(o c) -> o c", o=1))
+        ident = keep.tile([P, P], F32, name="ident")
+        make_identity(nc, ident[:])
         zcol = keep.tile([P, 1], F32, name="zcol")
         nc.vector.memset(zcol[:], 0.0)
         warm = keep.tile([P, 1], F32, name="warm")
@@ -54,25 +62,49 @@ def tile_treelstm_pa_kernel(tc, z_node, z_children, W_f, U_f, b_f, out_0, out_1)
 
         u_raw = keep.tile([P, 4, CH], BF16, name="u_raw")
         nc.sync.dma_start(out=u_raw[:], in_=U_f.rearrange("(t p) k -> p t k", p=P))
-        kid = []
-        node = []
+        hid, cel, node = {}, {}, {}
         for j in range(STEPS):
-            kid.append(keep.tile([P, 2, SIZE], BF16, name="kid%d" % j))
-            node.append(keep.tile([P, 2, SIZE], BF16, name="node%d" % j))
+            if j < SPLIT:
+                hid[j] = keep.tile([P, 2, CH], BF16, name="hid%d" % j)
+                cel[j] = keep.tile([P, 2, CH], BF16, name="cel%d" % j)
+            else:
+                hid[j] = keep.tile([P, 2, SIZE], BF16, name="kid%d" % j)
+            node[j] = keep.tile([P, 2, SIZE], BF16, name="node%d" % j)
 
-        def load(dst, src, j):
+        def rows(src, j):
             h, jj = divmod(j, STEPS_PER_HALF)
-            nc.sync.dma_start(out=dst[j][:], in_=src[h, :, 2 * jj : 2 * jj + 2, :])
+            return src[h, :, 2 * jj : 2 * jj + 2, :]
 
-        load(kid, zc, 0)
+        def load_hidden(j):
+            if j < SPLIT:
+                nc.sync.dma_start(out=hid[j][:], in_=rows(zc, j)[:, :, 0:CH])
+            else:
+                nc.sync.dma_start(out=hid[j][:], in_=rows(zc, j))
+
+        def load_cells(j):
+            nc.sync.dma_start(out=cel[j][:], in_=rows(zc, j)[:, :, CH:SIZE])
+
+        def load_node(j):
+            nc.sync.dma_start(out=node[j][:], in_=rows(zn, j))
+
+        def cells(j):
+            return cel[j][:] if j < SPLIT else hid[j][:, :, CH:SIZE]
+
+        load_hidden(0)
         w_raw = []
         for t in range(4):
             w_raw.append(keep.tile([P, SIZE], BF16, name="w_raw%d" % t))
             nc.sync.dma_start(out=w_raw[t][:], in_=W_f[t * P : (t + 1) * P, :])
-        load(node, zn, 0)
-        for j in range(1, STEPS):
-            load(node, zn, j)
-            load(kid, zc, j)
+        load_node(0)
+        load_hidden(1)
+        load_node(1)
+        load_cells(0)
+        load_hidden(2)
+        load_node(2)
+        load_cells(1)
+        for j in range(3, STEPS):
+            load_hidden(j)
+            load_node(j)
 
         def turn(dst, q, src):
             return lambda: nc.tensor.transpose(out=dst[:, q * P : (q + 1) * P], in_=src, identity=ident[:])
@@ -83,39 +115,28 @@ def tile_treelstm_pa_kernel(tc, z_node, z_children, W_f, U_f, b_f, out_0, out_1)
         def interleaved(src):
             return src[:].rearrange("p (g u r) -> p g r u", g=2, u=2)
 
-        u_words = u_raw[:].bitcast(F32)
-        ut = keep.tile([P, 4, CH], BF16, name="ut")
-        for u in range(2):
-            ps = bank("pl", 2)
-            run([turn(ps, t, u_words[:, t, P * u : P * (u + 1)]) for t in range(4)])
-            src = ps[:].bitcast(BF16).rearrange("p (c e) -> p e c", e=2)
-            if u == 0:
-                nc.vector.tensor_copy(out=ut[:, 0:2, :], in_=src)
-            else:
-                nc.scalar.copy(out=ut[:, 2:4, :], in_=src)
-
         zp, ht_ps, zt_ps, ht_sb, grouped, codes, scl = {}, {}, {}, {}, {}, {}, {}
-        pl_ps, mx_ps, tmp, s_sb, f_sb, p_sb = {}, {}, {}, {}, {}, {}
+        pl_ps, mx_ps, tmp, gates, p_sb = {}, {}, {}, {}, {}
         acc = [keep.tile([P, 2, CH], F32, name="acc%d" % h) for h in range(2)]
 
-        def permute(j):
+        def permute(j, copy):
             zp[j] = work.tile([P, 2 * SIZE], BF16, name="zp")
-            nc.scalar.copy(
+            copy(
                 out=zp[j][:].bitcast(F32).rearrange("p (q u i) -> p q u i", q=4, u=2),
                 in_=node[j][:].rearrange("p a k -> p (a k)").bitcast(F32).rearrange("p (q i u) -> p q u i", q=4, u=2),
             )
 
-        def transposes(j):
+        def turn_hidden(j):
             ht_ps[j] = bank("ht", 1)
-            kw = kid[j][:].bitcast(F32)
-            calls = [turn(ht_ps[j], 2 * a + u, kw[:, a, P * u : P * (u + 1)]) for a in range(2) for u in range(2)]
+            kw = hid[j][:].bitcast(F32)
+            return [turn(ht_ps[j], 2 * a + u, kw[:, a, P * u : P * (u + 1)]) for a in range(2) for u in range(2)]
+
+        def turn_node(j):
+            calls = []
+            words = zp[j][:].bitcast(F32)
             for a in range(2):
                 zt_ps[j, a] = bank("zt", 2)
-                if j in zp:
-                    words = zp[j][:].bitcast(F32)
-                    calls.extend([turn(zt_ps[j, a], q, words[:, (4 * a + q) * P : (4 * a + q + 1) * P]) for q in range(4)])
-                else:
-                    calls.extend(turn_every_2nd_word(zt_ps[j, a], node[j][:].bitcast(F32)[:, a, :]))
+                calls.extend([turn(zt_ps[j, a], q, words[:, (4 * a + q) * P : (4 * a + q + 1) * P]) for q in range(4)])
             return calls
 
         def evacuate_h(j):
@@ -137,9 +158,10 @@ def tile_treelstm_pa_kernel(tc, z_node, z_children, W_f, U_f, b_f, out_0, out_1)
                 out=codes[j][:].bitcast(FP8X4), scales=scl[j][:], in_=grouped[j][:].rearrange("p a k -> p (a k)")
             )
 
-        def plain(j, a, with_bias=False):
+        def plain(j, a):
             pl_ps[j, a] = bank("pl", 2)
             dst = pl_ps[j, a]
+            with_bias = j in BIASED
             calls = []
             if with_bias:
                 calls.append(lambda: nc.tensor.matmul(out=dst[:], lhsT=ones[:], rhs=brow[:], start=True, stop=False))
@@ -157,13 +179,12 @@ def tile_treelstm_pa_kernel(tc, z_node, z_children, W_f, U_f, b_f, out_0, out_1)
                 )
             return calls
 
-        def mx(j, a):
-            mx_ps[j, a] = bank("mx", 2)
+        def mx_part(dst, j, a, c0, c1):
             for g in range(2):
                 cols = slice((2 * a + g) * P, (2 * a + g + 1) * P)
-                wcols = slice(g * CH, (g + 1) * CH)
+                wcols = slice(g * CH + c0, g * CH + c1)
                 nc.tensor.matmul_mx(
-                    out=mx_ps[j, a][:],
+                    out=dst[:, 0 : c1 - c0],
                     lhsT=codes[j][:, cols].bitcast(FP8X4),
                     lhsT_scale=scl[j][:, cols],
                     rhs=wcodes[:, wcols].bitcast(FP8X4),
@@ -172,31 +193,35 @@ def tile_treelstm_pa_kernel(tc, z_node, z_children, W_f, U_f, b_f, out_0, out_1)
                     stop=(g == 1),
                 )
 
-        def add_bias(j, a):
-            tmp[j, a] = work.tile([P, CH], F32, name="tmp")
-            nc.vector.tensor_tensor(out=tmp[j, a][:], in0=pl_ps[j, a][:], in1=bias_sb[:], op=ALU.add)
+        def mx(j, a):
+            mx_ps[j, a] = bank("mx", 2)
+            mx_part(mx_ps[j, a], j, a, 0, CH)
 
-        def empty_plain(j, a):
-            tmp[j, a] = work.tile([P, CH], F32, name="tmp")
-            nc.scalar.copy(out=tmp[j, a][:], in_=pl_ps[j, a][:])
+        def plain_out(j, a):
+            tmp[j, a] = work.tile([P, CH], F32, name="tmp", bufs=4)
+            if j in BIASED:
+                nc.scalar.copy(out=tmp[j, a][:], in_=pl_ps[j, a][:])
+            else:
+                nc.vector.tensor_tensor(out=tmp[j, a][:], in0=pl_ps[j, a][:], in1=bias_sb[:], op=ALU.add)
 
         def add_mx(j, a):
-            s_sb[j, a] = work.tile([P, CH], F32, name="s%d" % a)
-            nc.vector.tensor_tensor(out=s_sb[j, a][:], in0=mx_ps[j, a][:], in1=tmp[j, a][:], op=ALU.add)
+            if a == 0:
+                gates[j] = work.tile([P, 2, CH], F32, name="gates")
+            nc.vector.tensor_tensor(out=gates[j][:, a, :], in0=mx_ps[j, a][:], in1=tmp[j, a][:], op=ALU.add)
 
         def gate(j, a):
-            f_sb[j, a] = work.tile([P, CH], F32, name="f%d" % a)
-            nc.scalar.activation(out=f_sb[j, a][:], in_=s_sb[j, a][:], func=ACT.Sigmoid)
+            nc.scalar.activation(out=gates[j][:, a, :], in_=gates[j][:, a, :], func=ACT.Sigmoid)
 
-        def times_cell(j, a):
+        def product_tile(j):
             h, jj = divmod(j, STEPS_PER_HALF)
             if jj == 0:
-                dst = acc[h]
-            else:
-                if a == 0:
-                    p_sb[j] = work.tile([P, 2, CH], F32, name="prod")
-                dst = p_sb[j]
-            nc.vector.tensor_tensor(out=dst[:, a, :], in0=f_sb[j, a][:], in1=kid[j][:, a, CH:SIZE], op=ALU.mult)
+                return acc[h]
+            if j not in p_sb:
+                p_sb[j] = work.tile([P, 2, CH], F32, name="prod")
+            return p_sb[j]
+
+        def times_cells(j):
+            nc.vector.tensor_tensor(out=product_tile(j)[:], in0=gates[j][:], in1=cells(j), op=ALU.mult)
 
         def accumulate(j, engine, cols):
             h, jj = divmod(j, STEPS_PER_HALF)
@@ -204,18 +229,46 @@ def tile_treelstm_pa_kernel(tc, z_node, z_children, W_f, U_f, b_f, out_0, out_1)
                 engine.tensor_tensor(out=acc[h][:, :, cols], in0=acc[h][:, :, cols], in1=p_sb[j][:, :, cols], op=ALU.add)
 
         o_sb = [keep.tile([P, CH], F32, name="o%d" % h) for h in range(2)]
-        part = keep.tile([P, 2], F32, name="part")
+        part = keep.tile([P, 3], F32, name="part")
 
-        def store_and_reduce(h):
-            nc.sync.dma_start(out=out_0[h * P : (h + 1) * P, :], in_=o_sb[h][:])
-            nc.vector.tensor_reduce(
-                out=part[:, h : h + 1], in_=o_sb[h][:], axis=AX.X, op=ALU.max, apply_absolute_value=True
-            )
+        def reduce_part(i, src):
+            nc.vector.tensor_reduce(out=part[:, i : i + 1], in_=src, axis=AX.X, op=ALU.max, apply_absolute_value=True)
 
-        def spread_part(h):
+        def spread_part(i):
             nc.tensor.transpose(
-                out=spread[:, h * P : (h + 1) * P], in_=part[:, h : h + 1].to_broadcast([P, P]), identity=ident[:]
+                out=spread[:, i * P : (i + 1) * P], in_=part[:, i : i + 1].to_broadcast([P, P]), identity=ident[:]
             )
+
+        def weave(mm, turns):
+            calls = []
+            nxt = 0
+            for i in range(len(mm)):
+                calls.append(mm[i])
+                take = WEAVE[i] if i < len(WEAVE) else 0
+                calls.extend(turns[nxt : nxt + take])
+                nxt += take
+            assert nxt >= len(turns)
+            return calls
+
+        bias_ps = bank("aux", 1)
+        for i in range(WARM):
+            nc.tensor.matmul(out=bias_ps[:], lhsT=ones[:], rhs=zeros[:], start=True, stop=True)
+
+        u_words = u_raw[:].bitcast(F32)
+        ut = keep.tile([P, 4, CH], BF16, name="ut")
+        for u in range(2):
+            ps = bank("pl", 2)
+            run([turn(ps, t, u_words[:, t, P * u : P * (u + 1)]) for t in range(4)])
+            src = ps[:].bitcast(BF16).rearrange("p (c e) -> p e c", e=2)
+            if u == 0:
+                nc.vector.tensor_copy(out=ut[:, 0:2, :], in_=src)
+            else:
+                nc.scalar.copy(out=ut[:, 2:4, :], in_=src)
+        nc.tensor.matmul(out=bias_ps[:], lhsT=ones[:], rhs=brow[:], start=True, stop=True)
+        bias_sb = keep.tile([P, CH], F32, name="bias_sb")
+        run(turn_hidden(0))
+        evacuate_h(0)
+        nc.scalar.copy(out=bias_sb[:], in_=bias_ps[:])
 
         wgrouped = keep.tile([P, 2, 4 * CH], BF16, name="wgrouped", align_bytes=64)
         wg_words = wgrouped[:].bitcast(F32).rearrange("p g (c u) -> p g c u", u=2)
@@ -231,18 +284,22 @@ def tile_treelstm_pa_kernel(tc, z_node, z_children, W_f, U_f, b_f, out_0, out_1)
             else:
                 nc.scalar.copy(out=dst, in_=interleaved(ps))
 
-        first = transposes(0)
-        run(first[0:4])
-        for t in range(4):
-            turn_w(t)
-        run(first[4:12])
-        bias_ps = bank("aux", 1)
-        nc.tensor.matmul(out=bias_ps[:], lhsT=ones[:], rhs=brow[:], start=True, stop=True)
-        bias_sb = keep.tile([P, CH], F32, name="bias_sb")
-        nc.vector.tensor_copy(out=bias_sb[:], in_=bias_ps[:])
-        evacuate_h(0)
+        turn_w(0)
+        turn_w(1)
+        run(plain(0, 0))
+        plain_out(0, 0)
+        turn_w(2)
+        pb = plain(0, 1)
+        run(pb[0:2])
+        permute(0, nc.vector.tensor_copy)
+        turn_w(3)
+        run(pb[2:4])
+        permute(1, nc.vector.tensor_copy)
+        plain_out(0, 1)
+        run(turn_hidden(1))
+        evacuate_h(1)
+        run(turn_node(0))
         evacuate_z(0)
-        permute(1)
         for g in range(2):
             wcols = slice(g * CH, (g + 1) * CH)
             nc.vector.quantize_mx(out=wcodes[:, wcols].bitcast(FP8X4), scales=wscl[:, wcols], in_=wgrouped[:, g, :])
@@ -250,59 +307,67 @@ def tile_treelstm_pa_kernel(tc, z_node, z_children, W_f, U_f, b_f, out_0, out_1)
 
         spread = bank("aux", 1)
         for j in range(LAST):
-            if j == STEPS_PER_HALF + 2:
+            if j == STEPS_PER_HALF + 4:
                 spread_part(0)
-            turns = transposes(j + 1)
-            pa = plain(j, 0)
-            pb = plain(j, 1)
-            run(pa + turns[0:6] + pb[0:2] + turns[6:12] + pb[2:4])
+            turns = (turn_hidden(j + 2) if j + 2 <= LAST else []) + turn_node(j + 1)
+            run(weave(plain(j + 1, 0) + plain(j + 1, 1), turns))
             mx(j, 0)
             mx(j, 1)
-            evacuate_h(j + 1)
-            evacuate_z(j + 1)
             if j + 2 <= LAST:
-                permute(j + 2)
-            add_bias(j, 0)
-            add_bias(j, 1)
+                permute(j + 2, nc.scalar.copy)
+                evacuate_h(j + 2)
+            evacuate_z(j + 1)
+            plain_out(j + 1, 0)
+            plain_out(j + 1, 1)
+            if j + 1 == LAST:
+                quantize(j + 1)
             add_mx(j, 0)
             add_mx(j, 1)
             gate(j, 0)
             gate(j, 1)
             if j >= 1:
                 accumulate(j - 1, nc.gpsimd, slice(0, G_COLS))
-            quantize(j + 1)
+            if j == STEPS_PER_HALF + 1:
+                nc.gpsimd.tensor_tensor(out=o_sb[0][:], in0=acc[0][:, 0, :], in1=acc[0][:, 1, :], op=ALU.add)
+            if j + 1 < LAST:
+                quantize(j + 1)
             if j >= 1:
                 accumulate(j - 1, nc.vector, slice(G_COLS, CH))
-            times_cell(j, 0)
-            times_cell(j, 1)
-            if j == STEPS_PER_HALF:
-                nc.vector.tensor_tensor(out=o_sb[0][:], in0=acc[0][:, 0, :], in1=acc[0][:, 1, :], op=ALU.add)
-                store_and_reduce(0)
+            times_cells(j)
+            if j == STEPS_PER_HALF + 1:
+                nc.sync.dma_start(out=out_0[0:P, :], in_=o_sb[0][:])
+                reduce_part(0, o_sb[0][:])
 
-        run(plain(LAST, 0, with_bias=True))
         mx(LAST, 0)
-        run(plain(LAST, 1, with_bias=True))
-        mx(LAST, 1)
-        accumulate(LAST - 1, nc.gpsimd, slice(0, G_COLS))
-        accumulate(LAST - 1, nc.vector, slice(G_COLS, CH))
-        empty_plain(LAST, 0)
+        halves = [slice(c * HALF, (c + 1) * HALF) for c in range(2)]
+        last_ps = []
+        for c in range(2):
+            last_ps.append(bank("zt", 2))
+            mx_part(last_ps[c], LAST, 1, c * HALF, (c + 1) * HALF)
+        accumulate(LAST - 1, nc.gpsimd, slice(0, TAIL_G_COLS))
         add_mx(LAST, 0)
         gate(LAST, 0)
-        empty_plain(LAST, 1)
-        times_cell(LAST, 0)
-        add_mx(LAST, 1)
-        gate(LAST, 1)
+        for c in range(2):
+            nc.vector.tensor_tensor(out=gates[LAST][:, 1, halves[c]], in0=last_ps[c][:, 0:HALF], in1=tmp[LAST, 1][:, halves[c]], op=ALU.add)
+            nc.scalar.activation(out=gates[LAST][:, 1, halves[c]], in_=gates[LAST][:, 1, halves[c]], func=ACT.Sigmoid)
+        accumulate(LAST - 1, nc.vector, slice(TAIL_G_COLS, CH))
+        prod = product_tile(LAST)
+        nc.vector.tensor_tensor(out=prod[:, 0, :], in0=gates[LAST][:, 0, :], in1=cells(LAST)[:, 0, :], op=ALU.mult)
         nc.vector.tensor_tensor(out=o_sb[1][:], in0=acc[1][:, 0, :], in1=acc[1][:, 1, :], op=ALU.add)
-        nc.vector.tensor_tensor(out=o_sb[1][:], in0=o_sb[1][:], in1=p_sb[LAST][:, 0, :], op=ALU.add)
-        times_cell(LAST, 1)
-        nc.vector.tensor_tensor(out=o_sb[1][:], in0=o_sb[1][:], in1=p_sb[LAST][:, 1, :], op=ALU.add)
-        store_and_reduce(1)
-        spread_part(1)
+        for c in range(2):
+            nc.vector.tensor_tensor(out=prod[:, 1, halves[c]], in0=gates[LAST][:, 1, halves[c]], in1=cells(LAST)[:, 1, halves[c]], op=ALU.mult)
+        nc.vector.tensor_tensor(out=o_sb[1][:], in0=o_sb[1][:], in1=prod[:, 0, :], op=ALU.add)
+        for c in range(2):
+            nc.vector.tensor_tensor(out=o_sb[1][:, halves[c]], in0=o_sb[1][:, halves[c]], in1=prod[:, 1, halves[c]], op=ALU.add)
+        nc.sync.dma_start(out=out_0[P : 2 * P, :], in_=o_sb[1][:])
+        for c in range(2):
+            reduce_part(1 + c, o_sb[1][:, halves[c]])
+            spread_part(1 + c)
 
-        junk = keep.tile([P, 2 * P], F32, name="junk")
+        junk = keep.tile([P, 3 * P], F32, name="junk")
         scale = keep.tile([P, 1], F32, name="scale")
         nc.vector.tensor_scalar(
-            out=junk[:], in0=spread[:, 0 : 2 * P], scalar1=1.0 / 448.0, scalar2=None, op0=ALU.mult, op1=ALU.max,
+            out=junk[:], in0=spread[:, 0 : 3 * P], scalar1=1.0 / 448.0, scalar2=None, op0=ALU.mult, op1=ALU.max,
             accum_out=scale[:, 0:1],
         )
         factor = keep.tile([P, 1], F32, name="factor")

@@ -46,13 +46,12 @@ def tile_treelstm_pa_kernel(tc, z_node, z_children, W_f, U_f, b_f, out_0, out_1)
             for call in calls:
                 call()
 
+        brow = keep.tile([P, CH], BF16, name="brow")
+        nc.vector.memset(brow[:], 0.0)
         ones = keep.tile([P, P], BF16, name="ones")
         nc.gpsimd.memset(ones[:], 1.0)
         zeros = keep.tile([P, CH], BF16, name="zeros")
         nc.vector.memset(zeros[:], 0.0)
-        brow = keep.tile([P, CH], BF16, name="brow")
-        nc.vector.memset(brow[:], 0.0)
-        nc.scalar.dma_start(out=brow[0:1, :], in_=b_f.rearrange("(o c) -> o c", o=1))
         ident = keep.tile([P, P], F32, name="ident")
         make_identity(nc, ident[:])
         zcol = keep.tile([P, 1], F32, name="zcol")
@@ -62,6 +61,7 @@ def tile_treelstm_pa_kernel(tc, z_node, z_children, W_f, U_f, b_f, out_0, out_1)
 
         u_raw = keep.tile([P, 4, CH], BF16, name="u_raw")
         nc.sync.dma_start(out=u_raw[:], in_=U_f.rearrange("(t p) k -> p t k", p=P))
+        nc.sync.dma_start(out=brow[0:1, :], in_=b_f.rearrange("(o c) -> o c", o=1))
         hid, cel, node = {}, {}, {}
         for j in range(STEPS):
             if j < SPLIT:
@@ -115,16 +115,9 @@ def tile_treelstm_pa_kernel(tc, z_node, z_children, W_f, U_f, b_f, out_0, out_1)
         def interleaved(src):
             return src[:].rearrange("p (g u r) -> p g r u", g=2, u=2)
 
-        zp, ht_ps, zt_ps, ht_sb, grouped, codes, scl = {}, {}, {}, {}, {}, {}, {}
+        ht_ps, zt_ps, ht_sb, grouped, codes, scl = {}, {}, {}, {}, {}, {}
         pl_ps, mx_ps, tmp, gates, p_sb = {}, {}, {}, {}, {}
         acc = [keep.tile([P, 2, CH], F32, name="acc%d" % h) for h in range(2)]
-
-        def permute(j, copy):
-            zp[j] = work.tile([P, 2 * SIZE], BF16, name="zp")
-            copy(
-                out=zp[j][:].bitcast(F32).rearrange("p (q u i) -> p q u i", q=4, u=2),
-                in_=node[j][:].rearrange("p a k -> p (a k)").bitcast(F32).rearrange("p (q i u) -> p q u i", q=4, u=2),
-            )
 
         def turn_hidden(j):
             ht_ps[j] = bank("ht", 1)
@@ -133,10 +126,9 @@ def tile_treelstm_pa_kernel(tc, z_node, z_children, W_f, U_f, b_f, out_0, out_1)
 
         def turn_node(j):
             calls = []
-            words = zp[j][:].bitcast(F32)
             for a in range(2):
                 zt_ps[j, a] = bank("zt", 2)
-                calls.extend([turn(zt_ps[j, a], q, words[:, (4 * a + q) * P : (4 * a + q + 1) * P]) for q in range(4)])
+                calls.extend(turn_every_2nd_word(zt_ps[j, a], node[j][:].bitcast(F32)[:, a, :]))
             return calls
 
         def evacuate_h(j):
@@ -220,8 +212,8 @@ def tile_treelstm_pa_kernel(tc, z_node, z_children, W_f, U_f, b_f, out_0, out_1)
                 p_sb[j] = work.tile([P, 2, CH], F32, name="prod")
             return p_sb[j]
 
-        def times_cells(j):
-            nc.vector.tensor_tensor(out=product_tile(j)[:], in0=gates[j][:], in1=cells(j), op=ALU.mult)
+        def times_cells(j, a):
+            nc.vector.tensor_tensor(out=product_tile(j)[:, a, :], in0=gates[j][:, a, :], in1=cells(j)[:, a, :], op=ALU.mult)
 
         def accumulate(j, engine, cols):
             h, jj = divmod(j, STEPS_PER_HALF)
@@ -291,10 +283,8 @@ def tile_treelstm_pa_kernel(tc, z_node, z_children, W_f, U_f, b_f, out_0, out_1)
         turn_w(2)
         pb = plain(0, 1)
         run(pb[0:2])
-        permute(0, nc.vector.tensor_copy)
         turn_w(3)
         run(pb[2:4])
-        permute(1, nc.vector.tensor_copy)
         plain_out(0, 1)
         run(turn_hidden(1))
         evacuate_h(1)
@@ -314,7 +304,6 @@ def tile_treelstm_pa_kernel(tc, z_node, z_children, W_f, U_f, b_f, out_0, out_1)
             mx(j, 0)
             mx(j, 1)
             if j + 2 <= LAST:
-                permute(j + 2, nc.scalar.copy)
                 evacuate_h(j + 2)
             evacuate_z(j + 1)
             plain_out(j + 1, 0)
@@ -333,7 +322,8 @@ def tile_treelstm_pa_kernel(tc, z_node, z_children, W_f, U_f, b_f, out_0, out_1)
                 quantize(j + 1)
             if j >= 1:
                 accumulate(j - 1, nc.vector, slice(G_COLS, CH))
-            times_cells(j)
+            times_cells(j, 0)
+            times_cells(j, 1)
             if j == STEPS_PER_HALF + 1:
                 nc.sync.dma_start(out=out_0[0:P, :], in_=o_sb[0][:])
                 reduce_part(0, o_sb[0][:])

@@ -20,11 +20,20 @@ STEPS = 16
 STEPS_PER_HALF = 8
 LAST = STEPS - 1
 HALF = CH // 2
-G_COLS = 384
+S_CAST = 384
+G_COLS_PER_READ = 96
 WARM = 6
 SPLIT = 2
-BIASED = (LAST,)
-WEAVE = (2, 2, 2, 2, 2, 1, 1, 0)
+BIAS_FROM = 6
+
+
+def biased(j, a):
+    return j == LAST or (a == 1 and j >= BIAS_FROM and j % 2 == 0)
+
+
+def g_cols(j):
+    return G_COLS_PER_READ * (2 + sum(1 for a in range(2) if not biased(j + 1, a)))
+WEAVE = (2, 2, 2, 2, 2, 1, 1, 0, 0, 0)
 TAIL_G_COLS = 128
 
 
@@ -153,7 +162,7 @@ def tile_treelstm_pa_kernel(tc, z_node, z_children, W_f, U_f, b_f, out_0, out_1)
         def plain(j, a):
             pl_ps[j, a] = bank("pl", 2)
             dst = pl_ps[j, a]
-            with_bias = j in BIASED
+            with_bias = biased(j, a)
             calls = []
             if with_bias:
                 calls.append(lambda: nc.tensor.matmul(out=dst[:], lhsT=ones[:], rhs=brow[:], start=True, stop=False))
@@ -191,7 +200,7 @@ def tile_treelstm_pa_kernel(tc, z_node, z_children, W_f, U_f, b_f, out_0, out_1)
 
         def plain_out(j, a):
             tmp[j, a] = work.tile([P, CH], F32, name="tmp", bufs=4)
-            if j in BIASED:
+            if biased(j, a):
                 nc.scalar.copy(out=tmp[j, a][:], in_=pl_ps[j, a][:])
             else:
                 nc.vector.tensor_tensor(out=tmp[j, a][:], in0=pl_ps[j, a][:], in1=bias_sb[:], op=ALU.add)
@@ -220,7 +229,8 @@ def tile_treelstm_pa_kernel(tc, z_node, z_children, W_f, U_f, b_f, out_0, out_1)
             if jj > 0:
                 engine.tensor_tensor(out=acc[h][:, :, cols], in0=acc[h][:, :, cols], in1=p_sb[j][:, :, cols], op=ALU.add)
 
-        o_sb = [keep.tile([P, CH], F32, name="o%d" % h) for h in range(2)]
+        o_all = keep.tile([P, 2, CH], F32, name="o_all")
+        o_sb = [o_all[:, h, :] for h in range(2)]
         part = keep.tile([P, 3], F32, name="part")
 
         def reduce_part(i, src):
@@ -315,18 +325,18 @@ def tile_treelstm_pa_kernel(tc, z_node, z_children, W_f, U_f, b_f, out_0, out_1)
             gate(j, 0)
             gate(j, 1)
             if j >= 1:
-                accumulate(j - 1, nc.gpsimd, slice(0, G_COLS))
+                accumulate(j - 1, nc.gpsimd, slice(0, g_cols(j)))
             if j == STEPS_PER_HALF + 1:
-                nc.gpsimd.tensor_tensor(out=o_sb[0][:], in0=acc[0][:, 0, :], in1=acc[0][:, 1, :], op=ALU.add)
+                nc.gpsimd.tensor_tensor(out=o_sb[0], in0=acc[0][:, 0, :], in1=acc[0][:, 1, :], op=ALU.add)
             if j + 1 < LAST:
                 quantize(j + 1)
             if j >= 1:
-                accumulate(j - 1, nc.vector, slice(G_COLS, CH))
+                accumulate(j - 1, nc.vector, slice(g_cols(j), CH))
             times_cells(j, 0)
             times_cells(j, 1)
             if j == STEPS_PER_HALF + 1:
-                nc.sync.dma_start(out=out_0[0:P, :], in_=o_sb[0][:])
-                reduce_part(0, o_sb[0][:])
+                nc.sync.dma_start(out=out_0[0:P, :], in_=o_sb[0])
+                reduce_part(0, o_sb[0])
 
         mx(LAST, 0)
         halves = [slice(c * HALF, (c + 1) * HALF) for c in range(2)]
@@ -343,13 +353,13 @@ def tile_treelstm_pa_kernel(tc, z_node, z_children, W_f, U_f, b_f, out_0, out_1)
         accumulate(LAST - 1, nc.vector, slice(TAIL_G_COLS, CH))
         prod = product_tile(LAST)
         nc.vector.tensor_tensor(out=prod[:, 0, :], in0=gates[LAST][:, 0, :], in1=cells(LAST)[:, 0, :], op=ALU.mult)
-        nc.vector.tensor_tensor(out=o_sb[1][:], in0=acc[1][:, 0, :], in1=acc[1][:, 1, :], op=ALU.add)
+        nc.vector.tensor_tensor(out=o_sb[1], in0=acc[1][:, 0, :], in1=acc[1][:, 1, :], op=ALU.add)
         for c in range(2):
             nc.vector.tensor_tensor(out=prod[:, 1, halves[c]], in0=gates[LAST][:, 1, halves[c]], in1=cells(LAST)[:, 1, halves[c]], op=ALU.mult)
-        nc.vector.tensor_tensor(out=o_sb[1][:], in0=o_sb[1][:], in1=prod[:, 0, :], op=ALU.add)
+        nc.vector.tensor_tensor(out=o_sb[1], in0=o_sb[1], in1=prod[:, 0, :], op=ALU.add)
         for c in range(2):
             nc.vector.tensor_tensor(out=o_sb[1][:, halves[c]], in0=o_sb[1][:, halves[c]], in1=prod[:, 1, halves[c]], op=ALU.add)
-        nc.sync.dma_start(out=out_0[P : 2 * P, :], in_=o_sb[1][:])
+        nc.sync.dma_start(out=out_0[P : 2 * P, :], in_=o_sb[1])
         for c in range(2):
             reduce_part(1 + c, o_sb[1][:, halves[c]])
             spread_part(1 + c)
@@ -363,10 +373,12 @@ def tile_treelstm_pa_kernel(tc, z_node, z_children, W_f, U_f, b_f, out_0, out_1)
         factor = keep.tile([P, 1], F32, name="factor")
         nc.vector.reciprocal(out=factor[:], in_=scale[:])
         o8 = keep.tile([P, 2, CH], FP8, name="o8")
+        o_flat = o_all[:].rearrange("p h c -> p (h c)")
+        o8_flat = o8[:].rearrange("p h c -> p (h c)")
         nc.vector.tensor_scalar(
-            out=o8[:, 1, :], in0=o_sb[1][:], scalar1=factor[:, 0:1], scalar2=None, op0=ALU.mult, saturate=False
+            out=o8_flat[:, S_CAST:], in0=o_flat[:, S_CAST:], scalar1=factor[:, 0:1], scalar2=None, op0=ALU.mult, saturate=False
         )
         nc.scalar.activation(
-            out=o8[:, 0, :], in_=o_sb[0][:], func=ACT.Identity, scale=factor[:, 0:1], bias=zcol[:, 0:1], saturate=False
+            out=o8_flat[:, 0:S_CAST], in_=o_flat[:, 0:S_CAST], func=ACT.Identity, scale=factor[:, 0:1], bias=zcol[:, 0:1], saturate=False
         )
         nc.sync.dma_start(out=out_1.rearrange("(h p) c -> p h c", p=P), in_=o8[:].bitcast(U8))

@@ -34,7 +34,7 @@ def biased(j, a):
 def g_cols(j):
     return G_COLS_PER_READ * (2 + sum(1 for a in range(2) if not biased(j + 1, a)))
 WEAVE = (2, 2, 2, 2, 2, 1, 1, 0, 0, 0)
-TAIL_G_COLS = 128
+LAST_ADDED = LAST - 3
 
 
 def tile_treelstm_pa_kernel(tc, z_node, z_children, W_f, U_f, b_f, out_0, out_1):
@@ -218,7 +218,7 @@ def tile_treelstm_pa_kernel(tc, z_node, z_children, W_f, U_f, b_f, out_0, out_1)
             if jj == 0:
                 return acc[h]
             if j not in p_sb:
-                p_sb[j] = work.tile([P, 2, CH], F32, name="prod")
+                p_sb[j] = work.tile([P, 2, CH], F32, name="prod", bufs=3)
             return p_sb[j]
 
         def times_cells(j, a):
@@ -324,16 +324,17 @@ def tile_treelstm_pa_kernel(tc, z_node, z_children, W_f, U_f, b_f, out_0, out_1)
             add_mx(j, 1)
             gate(j, 0)
             gate(j, 1)
-            if j >= 1:
+            if 1 <= j <= LAST_ADDED + 1:
                 accumulate(j - 1, nc.gpsimd, slice(0, g_cols(j)))
             if j == STEPS_PER_HALF + 1:
                 nc.gpsimd.tensor_tensor(out=o_sb[0], in0=acc[0][:, 0, :], in1=acc[0][:, 1, :], op=ALU.add)
             if j + 1 < LAST:
                 quantize(j + 1)
-            if j >= 1:
+            if 1 <= j <= LAST_ADDED + 1:
                 accumulate(j - 1, nc.vector, slice(g_cols(j), CH))
             times_cells(j, 0)
-            times_cells(j, 1)
+            if j + 1 < LAST:
+                times_cells(j, 1)
             if j == STEPS_PER_HALF + 1:
                 nc.sync.dma_start(out=out_0[0:P, :], in_=o_sb[0])
                 reduce_part(0, o_sb[0])
@@ -344,25 +345,51 @@ def tile_treelstm_pa_kernel(tc, z_node, z_children, W_f, U_f, b_f, out_0, out_1)
         for c in range(2):
             last_ps.append(bank("zt", 2))
             mx_part(last_ps[c], LAST, 1, c * HALF, (c + 1) * HALF)
-        accumulate(LAST - 1, nc.gpsimd, slice(0, TAIL_G_COLS))
+        prod = product_tile(LAST)
+
+        o_t = [bank("pl", 2), bank("pl", 2)]
+
+        def add_turned(src, c, first=False, last=False):
+            for i in range(2):
+                nc.tensor.matmul(
+                    out=o_t[c][:, i * P : (i + 1) * P],
+                    lhsT=src[:, (2 * c + i) * P : (2 * c + i + 1) * P],
+                    rhs=ident[:],
+                    is_transpose=True,
+                    start=(first and i == 0),
+                    stop=(last and i == 1),
+                )
+
         add_mx(LAST, 0)
         gate(LAST, 0)
         for c in range(2):
             nc.vector.tensor_tensor(out=gates[LAST][:, 1, halves[c]], in0=last_ps[c][:, 0:HALF], in1=tmp[LAST, 1][:, halves[c]], op=ALU.add)
             nc.scalar.activation(out=gates[LAST][:, 1, halves[c]], in_=gates[LAST][:, 1, halves[c]], func=ACT.Sigmoid)
-        accumulate(LAST - 1, nc.vector, slice(TAIL_G_COLS, CH))
-        prod = product_tile(LAST)
+        times_cells(LAST - 1, 1)
+        for a in range(2):
+            for c in range(2):
+                add_turned(acc[1][:, a, :], c, first=(a == 0))
+        for j in range(LAST_ADDED + 1, LAST):
+            for a in range(2):
+                for c in range(2):
+                    add_turned(p_sb[j][:, a, :], c)
         nc.vector.tensor_tensor(out=prod[:, 0, :], in0=gates[LAST][:, 0, :], in1=cells(LAST)[:, 0, :], op=ALU.mult)
-        nc.vector.tensor_tensor(out=o_sb[1], in0=acc[1][:, 0, :], in1=acc[1][:, 1, :], op=ALU.add)
+        for c in range(2):
+            add_turned(prod[:, 0, :], c)
+        ot_sb = keep.tile([P, CH], F32, name="ot_sb")
+        back = bank("ht", 1)
         for c in range(2):
             nc.vector.tensor_tensor(out=prod[:, 1, halves[c]], in0=gates[LAST][:, 1, halves[c]], in1=cells(LAST)[:, 1, halves[c]], op=ALU.mult)
-        nc.vector.tensor_tensor(out=o_sb[1], in0=o_sb[1], in1=prod[:, 0, :], op=ALU.add)
+            add_turned(prod[:, 1, :], c, last=True)
         for c in range(2):
-            nc.vector.tensor_tensor(out=o_sb[1][:, halves[c]], in0=o_sb[1][:, halves[c]], in1=prod[:, 1, halves[c]], op=ALU.add)
-        nc.sync.dma_start(out=out_0[P : 2 * P, :], in_=o_sb[1])
-        for c in range(2):
-            reduce_part(1 + c, o_sb[1][:, halves[c]])
+            nc.scalar.copy(out=ot_sb[:, halves[c]], in_=o_t[c][:, 0:HALF])
+            reduce_part(1 + c, ot_sb[:, halves[c]])
+            for i in range(2):
+                blk = slice((2 * c + i) * P, (2 * c + i + 1) * P)
+                nc.tensor.transpose(out=back[:, blk], in_=ot_sb[:, blk], identity=ident[:])
             spread_part(1 + c)
+        nc.scalar.copy(out=o_sb[1], in_=back[:])
+        nc.sync.dma_start(out=out_0[P : 2 * P, :], in_=o_sb[1])
 
         junk = keep.tile([P, 3 * P], F32, name="junk")
         scale = keep.tile([P, 1], F32, name="scale")

@@ -265,7 +265,8 @@ def tile_treelstm_pa_kernel(tc, z_node, z_children, W_f, U_f, b_f, out_0, out_1)
             if u == 0:
                 nc.vector.tensor_copy(out=ut[:, 0:2, :], in_=src)
             else:
-                nc.scalar.copy(out=ut[:, 2:4, :], in_=src)
+                nc.scalar.copy(out=ut[:, 2:3, :], in_=src[:, 0:1, :])
+                nc.vector.tensor_copy(out=ut[:, 3:4, :], in_=src[:, 1:2, :])
         nc.tensor.matmul(out=bias_ps[:], lhsT=ones[:], rhs=brow[:], start=True, stop=True)
         bias_sb = keep.tile([P, CH], F32, name="bias_sb")
         run(turn_hidden(0))
@@ -294,10 +295,10 @@ def tile_treelstm_pa_kernel(tc, z_node, z_children, W_f, U_f, b_f, out_0, out_1)
         pb = plain(0, 1)
         run(pb[0:2])
         turn_w(3)
-        run(pb[2:4])
-        plain_out(0, 1)
         run(turn_hidden(1))
         evacuate_h(1)
+        run(pb[2:4])
+        plain_out(0, 1)
         run(turn_node(0))
         evacuate_z(0)
         for g in range(2):
@@ -307,8 +308,6 @@ def tile_treelstm_pa_kernel(tc, z_node, z_children, W_f, U_f, b_f, out_0, out_1)
 
         spread = bank("aux", 1)
         for j in range(LAST):
-            if j == STEPS_PER_HALF + 4:
-                spread_part(0)
             turns = (turn_hidden(j + 2) if j + 2 <= LAST else []) + turn_node(j + 1)
             run(weave(plain(j + 1, 0) + plain(j + 1, 1), turns))
             mx(j, 0)
@@ -332,14 +331,14 @@ def tile_treelstm_pa_kernel(tc, z_node, z_children, W_f, U_f, b_f, out_0, out_1)
                 quantize(j + 1)
             if 1 <= j <= LAST_ADDED + 1:
                 accumulate(j - 1, nc.vector, slice(g_cols(j), CH))
-            times_cells(j, 0)
             if j + 1 < LAST:
+                times_cells(j, 0)
                 times_cells(j, 1)
             if j == STEPS_PER_HALF + 1:
                 nc.sync.dma_start(out=out_0[0:P, :], in_=o_sb[0])
-                reduce_part(0, o_sb[0])
 
-        mx(LAST, 0)
+        mx_ps[LAST, 0] = bank("ht", 1)
+        mx_part(mx_ps[LAST, 0], LAST, 0, 0, CH)
         halves = [slice(c * HALF, (c + 1) * HALF) for c in range(2)]
         last_ps = []
         for c in range(2):
@@ -365,6 +364,7 @@ def tile_treelstm_pa_kernel(tc, z_node, z_children, W_f, U_f, b_f, out_0, out_1)
         for c in range(2):
             nc.vector.tensor_tensor(out=gates[LAST][:, 1, halves[c]], in0=last_ps[c][:, 0:HALF], in1=tmp[LAST, 1][:, halves[c]], op=ALU.add)
             nc.scalar.activation(out=gates[LAST][:, 1, halves[c]], in_=gates[LAST][:, 1, halves[c]], func=ACT.Sigmoid)
+        times_cells(LAST - 1, 0)
         times_cells(LAST - 1, 1)
         for a in range(2):
             for c in range(2):
@@ -377,10 +377,14 @@ def tile_treelstm_pa_kernel(tc, z_node, z_children, W_f, U_f, b_f, out_0, out_1)
         for c in range(2):
             add_turned(prod[:, 0, :], c)
         ot_sb = keep.tile([P, CH], F32, name="ot_sb")
-        back = bank("ht", 1)
+        back = bank("mx", 2)
         for c in range(2):
             nc.vector.tensor_tensor(out=prod[:, 1, halves[c]], in0=gates[LAST][:, 1, halves[c]], in1=cells(LAST)[:, 1, halves[c]], op=ALU.mult)
             add_turned(prod[:, 1, :], c, last=True)
+        reduce_part(0, o_sb[0])
+        spread_part(0)
+        junk = keep.tile([P, 3 * P], F32, name="junk")
+        scale0 = keep.tile([P, 1], F32, name="scale0")
         for c in range(2):
             nc.scalar.copy(out=ot_sb[:, halves[c]], in_=o_t[c][:, 0:HALF])
             reduce_part(1 + c, ot_sb[:, halves[c]])
@@ -388,13 +392,15 @@ def tile_treelstm_pa_kernel(tc, z_node, z_children, W_f, U_f, b_f, out_0, out_1)
                 blk = slice((2 * c + i) * P, (2 * c + i + 1) * P)
                 nc.tensor.transpose(out=back[:, blk], in_=ot_sb[:, blk], identity=ident[:])
             spread_part(1 + c)
+        nc.vector.tensor_scalar(
+            out=junk[:, 0:P], in0=spread[:, 0:P], scalar1=1.0 / 448.0, scalar2=None, op0=ALU.mult, op1=ALU.max, accum_out=scale0[:, 0:1]
+        )
         nc.scalar.copy(out=o_sb[1], in_=back[:])
         nc.sync.dma_start(out=out_0[P : 2 * P, :], in_=o_sb[1])
 
-        junk = keep.tile([P, 3 * P], F32, name="junk")
         scale = keep.tile([P, 1], F32, name="scale")
         nc.vector.tensor_scalar(
-            out=junk[:], in0=spread[:, 0 : 3 * P], scalar1=1.0 / 448.0, scalar2=None, op0=ALU.mult, op1=ALU.max,
+            out=junk[:, P : 3 * P], in0=spread[:, P : 3 * P], scalar1=1.0 / 448.0, scalar2=scale0[:, 0:1], op0=ALU.mult, op1=ALU.max,
             accum_out=scale[:, 0:1],
         )
         factor = keep.tile([P, 1], F32, name="factor")

@@ -24,7 +24,7 @@ S_CAST = 384
 G_COLS_PER_READ = 96
 WARM = 6
 SPLIT = 2
-BIAS_FROM = 6
+BIAS_FROM = 2
 
 
 def biased(j, a):
@@ -34,7 +34,7 @@ def biased(j, a):
 def g_cols(j):
     return G_COLS_PER_READ * (2 + sum(1 for a in range(2) if not biased(j + 1, a)))
 WEAVE = (2, 2, 2, 2, 2, 1, 1, 0, 0, 0)
-LAST_ADDED = LAST - 3
+LAST_ADDED = LAST - 4
 
 
 def tile_treelstm_pa_kernel(tc, z_node, z_children, W_f, U_f, b_f, out_0, out_1):
@@ -218,7 +218,7 @@ def tile_treelstm_pa_kernel(tc, z_node, z_children, W_f, U_f, b_f, out_0, out_1)
             if jj == 0:
                 return acc[h]
             if j not in p_sb:
-                p_sb[j] = work.tile([P, 2, CH], F32, name="prod", bufs=3)
+                p_sb[j] = work.tile([P, 2, CH], F32, name="prod", bufs=4)
             return p_sb[j]
 
         def times_cells(j, a):

@@ -33,7 +33,6 @@ def biased(j, a):
 
 def g_cols(j):
     return G_COLS_PER_READ * (2 + sum(1 for a in range(2) if not biased(j + 1, a)))
-WEAVE = (2, 2, 2, 2, 2, 1, 1, 0, 0, 0)
 LAST_ADDED = LAST - 4
 
 
@@ -241,15 +240,18 @@ def tile_treelstm_pa_kernel(tc, z_node, z_children, W_f, U_f, b_f, out_0, out_1)
                 out=spread[:, i * P : (i + 1) * P], in_=part[:, i : i + 1].to_broadcast([P, P]), identity=ident[:]
             )
 
-        def weave(mm, turns):
+        def weave(mm, z_turns, h_turns):
+            gaps = len(mm) - 1
             calls = []
-            nxt = 0
-            for i in range(len(mm)):
+            z_next = 0
+            for i in range(gaps):
                 calls.append(mm[i])
-                take = WEAVE[i] if i < len(WEAVE) else 0
-                calls.extend(turns[nxt : nxt + take])
-                nxt += take
-            assert nxt >= len(turns)
+                take = len(z_turns) - z_next if i == gaps - 1 else min(1, len(z_turns) - z_next)
+                calls.extend(z_turns[z_next : z_next + take])
+                z_next += take
+                calls.extend(h_turns[i : i + 1])
+            assert len(h_turns) <= gaps
+            calls.append(mm[gaps])
             return calls
 
         bias_ps = bank("aux", 1)
@@ -308,8 +310,8 @@ def tile_treelstm_pa_kernel(tc, z_node, z_children, W_f, U_f, b_f, out_0, out_1)
 
         spread = bank("aux", 1)
         for j in range(LAST):
-            turns = (turn_hidden(j + 2) if j + 2 <= LAST else []) + turn_node(j + 1)
-            run(weave(plain(j + 1, 0) + plain(j + 1, 1), turns))
+            h_turns = turn_hidden(j + 2) if j + 2 <= LAST else []
+            run(weave(plain(j + 1, 0) + plain(j + 1, 1), turn_node(j + 1), h_turns))
             mx(j, 0)
             mx(j, 1)
             if j + 2 <= LAST:

@@ -21,7 +21,7 @@ STEPS_PER_HALF = 8
 LAST = STEPS - 1
 HALF = CH // 2
 S_CAST = 384
-G_COLS_PER_READ = 96
+G_COLS_PER_READ = 108
 WARM = 6
 SPLIT = 2
 BIAS_FROM = 2
@@ -32,7 +32,7 @@ def biased(j, a):
 
 
 def g_cols(j):
-    return G_COLS_PER_READ * (2 + sum(1 for a in range(2) if not biased(j + 1, a)))
+    return G_COLS_PER_READ * (2 + sum(1 for a in range(2) if not biased(j + 1, a))) // 16 * 16
 LAST_ADDED = LAST - 4
 
 
@@ -223,10 +223,10 @@ def tile_treelstm_pa_kernel(tc, z_node, z_children, W_f, U_f, b_f, out_0, out_1)
         def times_cells(j, a):
             nc.vector.tensor_tensor(out=product_tile(j)[:, a, :], in0=gates[j][:, a, :], in1=cells(j)[:, a, :], op=ALU.mult)
 
-        def accumulate(j, engine, cols):
+        def accumulate(j, engine, cols, tiles=slice(0, 2)):
             h, jj = divmod(j, STEPS_PER_HALF)
             if jj > 0:
-                engine.tensor_tensor(out=acc[h][:, :, cols], in0=acc[h][:, :, cols], in1=p_sb[j][:, :, cols], op=ALU.add)
+                engine.tensor_tensor(out=acc[h][:, tiles, cols], in0=acc[h][:, tiles, cols], in1=p_sb[j][:, tiles, cols], op=ALU.add)
 
         o_all = keep.tile([P, 2, CH], F32, name="o_all")
         o_sb = [o_all[:, h, :] for h in range(2)]
@@ -326,7 +326,8 @@ def tile_treelstm_pa_kernel(tc, z_node, z_children, W_f, U_f, b_f, out_0, out_1)
             gate(j, 0)
             gate(j, 1)
             if 1 <= j <= LAST_ADDED + 1:
-                accumulate(j - 1, nc.gpsimd, slice(0, g_cols(j)))
+                for a in range(2):
+                    accumulate(j - 1, nc.gpsimd, slice(0, g_cols(j)), slice(a, a + 1))
             if j == STEPS_PER_HALF + 1:
                 nc.gpsimd.tensor_tensor(out=o_sb[0], in0=acc[0][:, 0, :], in1=acc[0][:, 1, :], op=ALU.add)
             if j + 1 < LAST:

from contextlib import ExitStack

import concourse.mybir as mybir
from concourse.masks import make_identity

F32 = mybir.dt.float32
BF16 = mybir.dt.bfloat16
U32 = mybir.dt.uint32
U8 = mybir.dt.uint8
FP8X4 = mybir.dt.float8_e4m3fn_x4
FP8 = mybir.dt.float8_e4m3fn
ALU = mybir.AluOpType
ACT = mybir.ActivationFunctionType
AX = mybir.AxisListType

P = 128
NODES, KIDS, SIZE, CH = 256, 16, 1024, 512
FLOPS = 2 * NODES * KIDS * CH * (SIZE + CH)
STEPS = 16
STEPS_PER_HALF = 8
LAST = STEPS - 1
HALF = CH // 2
S_CAST = 384
G_COLS_PER_READ = 108
WARM = 6
SPLIT = 2
BIAS_FROM = 2


def biased(j, a):
    return j == LAST or (a == 1 and j >= BIAS_FROM and j % 2 == 0)


def g_cols(j):
    return G_COLS_PER_READ * (2 + sum(1 for a in range(2) if not biased(j + 1, a))) // 16 * 16
LAST_ADDED = LAST - 4


def tile_treelstm_pa_kernel(tc, z_node, z_children, W_f, U_f, b_f, out_0, out_1):
    nc = tc.nc
    zn = z_node.rearrange("(h p) n k -> h p n k", p=P)
    zc = z_children.rearrange("(h p) n k -> h p n k", p=P)

    with ExitStack() as ctx:
        keep = ctx.enter_context(tc.tile_pool(name="keep", bufs=1))
        work = ctx.enter_context(tc.tile_pool(name="work", bufs=2))
        psum = ctx.enter_context(tc.psum_pool(name="psum", bufs=2))
        ctx.enter_context(tc.manual_schedule())

        def bank(tag, bufs):
            return psum.tile([P, 512], F32, name=tag, bufs=bufs)

        def run(calls):
            for call in calls:
                call()

        brow = keep.tile([P, CH], BF16, name="brow")
        nc.vector.memset(brow[:], 0.0)
        ones = keep.tile([P, P], BF16, name="ones")
        nc.gpsimd.memset(ones[:], 1.0)
        zeros = keep.tile([P, CH], BF16, name="zeros")
        nc.vector.memset(zeros[:], 0.0)
        ident = keep.tile([P, P], F32, name="ident")
        make_identity(nc, ident[:])
        zcol = keep.tile([P, 1], F32, name="zcol")
        nc.vector.memset(zcol[:], 0.0)
        warm = keep.tile([P, 1], F32, name="warm")
        nc.scalar.activation(out=warm[:], in_=zcol[:], func=ACT.Sigmoid)

        u_raw = keep.tile([P, 4, CH], BF16, name="u_raw")
        nc.sync.dma_start(out=u_raw[:], in_=U_f.rearrange("(t p) k -> p t k", p=P))
        nc.sync.dma_start(out=brow[0:1, :], in_=b_f.rearrange("(o c) -> o c", o=1))
        hid, cel, node = {}, {}, {}
        for j in range(STEPS):
            if j < SPLIT:
                hid[j] = keep.tile([P, 2, CH], BF16, name="hid%d" % j)
                cel[j] = keep.tile([P, 2, CH], BF16, name="cel%d" % j)
            else:
                hid[j] = keep.tile([P, 2, SIZE], BF16, name="kid%d" % j)
            node[j] = keep.tile([P, 2, SIZE], BF16, name="node%d" % j)

        def rows(src, j):
            h, jj = divmod(j, STEPS_PER_HALF)
            return src[h, :, 2 * jj : 2 * jj + 2, :]

        def load_hidden(j):
            if j < SPLIT:
                nc.sync.dma_start(out=hid[j][:], in_=rows(zc, j)[:, :, 0:CH])
            else:
                nc.sync.dma_start(out=hid[j][:], in_=rows(zc, j))

        def load_cells(j):
            nc.sync.dma_start(out=cel[j][:], in_=rows(zc, j)[:, :, CH:SIZE])

        def load_node(j):
            nc.sync.dma_start(out=node[j][:], in_=rows(zn, j))

        def cells(j):
            return cel[j][:] if j < SPLIT else hid[j][:, :, CH:SIZE]

        load_hidden(0)
        w_raw = []
        for t in range(4):
            w_raw.append(keep.tile([P, SIZE], BF16, name="w_raw%d" % t))
            nc.sync.dma_start(out=w_raw[t][:], in_=W_f[t * P : (t + 1) * P, :])
        load_node(0)
        load_hidden(1)
        load_node(1)
        load_cells(0)
        load_hidden(2)
        load_node(2)
        load_cells(1)
        for j in range(3, STEPS):
            load_hidden(j)
            load_node(j)

        def turn(dst, q, src):
            return lambda: nc.tensor.transpose(out=dst[:, q * P : (q + 1) * P], in_=src, identity=ident[:])

        def turn_every_2nd_word(dst, words):
            return [turn(dst, 2 * g + u, words[:, 256 * g + u : 256 * (g + 1) : 2]) for g in range(2) for u in range(2)]

        def interleaved(src):
            return src[:].rearrange("p (g u r) -> p g r u", g=2, u=2)

        ht_ps, zt_ps, ht_sb, grouped, codes, scl = {}, {}, {}, {}, {}, {}
        pl_ps, mx_ps, tmp, gates, p_sb = {}, {}, {}, {}, {}
        acc = [keep.tile([P, 2, CH], F32, name="acc%d" % h) for h in range(2)]

        def turn_hidden(j):
            ht_ps[j] = bank("ht", 1)
            kw = hid[j][:].bitcast(F32)
            return [turn(ht_ps[j], 2 * a + u, kw[:, a, P * u : P * (u + 1)]) for a in range(2) for u in range(2)]

        def turn_node(j):
            calls = []
            for a in range(2):
                zt_ps[j, a] = bank("zt", 2)
                calls.extend(turn_every_2nd_word(zt_ps[j, a], node[j][:].bitcast(F32)[:, a, :]))
            return calls

        def evacuate_h(j):
            ht_sb[j] = work.tile([P, 2 * CH], BF16, name="ht_sb")
            nc.scalar.copy(out=ht_sb[j][:].bitcast(F32), in_=ht_ps[j][:])

        def evacuate_z(j):
            grouped[j] = work.tile([P, 2, SIZE], BF16, name="grouped", align_bytes=64)
            for a in range(2):
                nc.scalar.copy(
                    out=grouped[j][:, a, :].bitcast(F32).rearrange("p (g r u) -> p g r u", g=2, u=2),
                    in_=interleaved(zt_ps[j, a]),
                )

        def quantize(j):
            codes[j] = work.tile([P, 4 * P], U32, name="codes", align_bytes=64)
            scl[j] = work.tile([P, 4 * P], U8, name="scl", align_bytes=64)
            nc.vector.quantize_mx(
                out=codes[j][:].bitcast(FP8X4), scales=scl[j][:], in_=grouped[j][:].rearrange("p a k -> p (a k)")
            )

        def plain(j, a):
            pl_ps[j, a] = bank("pl", 2)
            dst = pl_ps[j, a]
            with_bias = biased(j, a)
            calls = []
            if with_bias:
                calls.append(lambda: nc.tensor.matmul(out=dst[:], lhsT=ones[:], rhs=brow[:], start=True, stop=False))
            for q in range(4):
                u, e = divmod(q, 2)
                base = (2 * a + u) * 256
                calls.append(
                    lambda q=q, base=base, e=e: nc.tensor.matmul(
                        out=dst[:],
                        lhsT=ht_sb[j][:, base + e : base + 256 : 2],
                        rhs=ut[:, q, :],
                        start=(q == 0 and not with_bias),
                        stop=(q == 3),
                    )
                )
            return calls

        def mx_part(dst, j, a, c0, c1):
            for g in range(2):
                cols = slice((2 * a + g) * P, (2 * a + g + 1) * P)
                wcols = slice(g * CH + c0, g * CH + c1)
                nc.tensor.matmul_mx(
                    out=dst[:, 0 : c1 - c0],
                    lhsT=codes[j][:, cols].bitcast(FP8X4),
                    lhsT_scale=scl[j][:, cols],
                    rhs=wcodes[:, wcols].bitcast(FP8X4),
                    rhs_scale=wscl[:, wcols],
                    start=(g == 0),
                    stop=(g == 1),
                )

        def mx(j, a):
            mx_ps[j, a] = bank("mx", 2)
            mx_part(mx_ps[j, a], j, a, 0, CH)

        def plain_out(j, a):
            tmp[j, a] = work.tile([P, CH], F32, name="tmp", bufs=4)
            if biased(j, a):
                nc.scalar.copy(out=tmp[j, a][:], in_=pl_ps[j, a][:])
            else:
                nc.vector.tensor_tensor(out=tmp[j, a][:], in0=pl_ps[j, a][:], in1=bias_sb[:], op=ALU.add)

        def add_mx(j, a):
            if a == 0:
                gates[j] = work.tile([P, 2, CH], F32, name="gates")
            nc.vector.tensor_tensor(out=gates[j][:, a, :], in0=mx_ps[j, a][:], in1=tmp[j, a][:], op=ALU.add)

        def gate(j, a):
            nc.scalar.activation(out=gates[j][:, a, :], in_=gates[j][:, a, :], func=ACT.Sigmoid)

        def product_tile(j):
            h, jj = divmod(j, STEPS_PER_HALF)
            if jj == 0:
                return acc[h]
            if j not in p_sb:
                p_sb[j] = work.tile([P, 2, CH], F32, name="prod", bufs=4)
            return p_sb[j]

        def times_cells(j, a):
            nc.vector.tensor_tensor(out=product_tile(j)[:, a, :], in0=gates[j][:, a, :], in1=cells(j)[:, a, :], op=ALU.mult)

        def accumulate(j, engine, cols, tiles=slice(0, 2)):
            h, jj = divmod(j, STEPS_PER_HALF)
            if jj > 0:
                engine.tensor_tensor(out=acc[h][:, tiles, cols], in0=acc[h][:, tiles, cols], in1=p_sb[j][:, tiles, cols], op=ALU.add)

        o_all = keep.tile([P, 2, CH], F32, name="o_all")
        o_sb = [o_all[:, h, :] for h in range(2)]
        part = keep.tile([P, 3], F32, name="part")

        def reduce_part(i, src):
            nc.vector.tensor_reduce(out=part[:, i : i + 1], in_=src, axis=AX.X, op=ALU.max, apply_absolute_value=True)

        def spread_part(i):
            nc.tensor.transpose(
                out=spread[:, i * P : (i + 1) * P], in_=part[:, i : i + 1].to_broadcast([P, P]), identity=ident[:]
            )

        def weave(mm, z_turns, h_turns):
            gaps = len(mm) - 1
            calls = []
            z_next = 0
            for i in range(gaps):
                calls.append(mm[i])
                take = len(z_turns) - z_next if i == gaps - 1 else min(1, len(z_turns) - z_next)
                calls.extend(z_turns[z_next : z_next + take])
                z_next += take
                calls.extend(h_turns[i : i + 1])
            assert len(h_turns) <= gaps
            calls.append(mm[gaps])
            return calls

        bias_ps = bank("aux", 1)
        for i in range(WARM):
            nc.tensor.matmul(out=bias_ps[:], lhsT=ones[:], rhs=zeros[:], start=True, stop=True)

        u_words = u_raw[:].bitcast(F32)
        ut = keep.tile([P, 4, CH], BF16, name="ut")
        for u in range(2):
            ps = bank("pl", 2)
            run([turn(ps, t, u_words[:, t, P * u : P * (u + 1)]) for t in range(4)])
            src = ps[:].bitcast(BF16).rearrange("p (c e) -> p e c", e=2)
            if u == 0:
                nc.vector.tensor_copy(out=ut[:, 0:2, :], in_=src)
            else:
                nc.scalar.copy(out=ut[:, 2:3, :], in_=src[:, 0:1, :])
                nc.vector.tensor_copy(out=ut[:, 3:4, :], in_=src[:, 1:2, :])
        nc.tensor.matmul(out=bias_ps[:], lhsT=ones[:], rhs=brow[:], start=True, stop=True)
        bias_sb = keep.tile([P, CH], F32, name="bias_sb")
        run(turn_hidden(0))
        evacuate_h(0)
        nc.scalar.copy(out=bias_sb[:], in_=bias_ps[:])

        wgrouped = keep.tile([P, 2, 4 * CH], BF16, name="wgrouped", align_bytes=64)
        wg_words = wgrouped[:].bitcast(F32).rearrange("p g (c u) -> p g c u", u=2)
        wcodes = keep.tile([P, 2 * CH], U32, name="wcodes", align_bytes=64)
        wscl = keep.tile([P, 2 * CH], U8, name="wscl", align_bytes=64)

        def turn_w(t):
            ps = bank("mx", 2)
            run(turn_every_2nd_word(ps, w_raw[t][:].bitcast(F32)))
            dst = wg_words[:, :, t * P : (t + 1) * P, :]
            if t % 2 == 0:
                nc.vector.tensor_copy(out=dst, in_=interleaved(ps))
            else:
                nc.scalar.copy(out=dst, in_=interleaved(ps))

        turn_w(0)
        turn_w(1)
        run(plain(0, 0))
        plain_out(0, 0)
        turn_w(2)
        pb = plain(0, 1)
        run(pb[0:2])
        turn_w(3)
        run(turn_hidden(1))
        evacuate_h(1)
        run(pb[2:4])
        plain_out(0, 1)
        run(turn_node(0))
        evacuate_z(0)
        for g in range(2):
            wcols = slice(g * CH, (g + 1) * CH)
            nc.vector.quantize_mx(out=wcodes[:, wcols].bitcast(FP8X4), scales=wscl[:, wcols], in_=wgrouped[:, g, :])
        quantize(0)

        spread = bank("aux", 1)
        for j in range(LAST):
            h_turns = turn_hidden(j + 2) if j + 2 <= LAST else []
            run(weave(plain(j + 1, 0) + plain(j + 1, 1), turn_node(j + 1), h_turns))
            mx(j, 0)
            mx(j, 1)
            if j + 2 <= LAST:
                evacuate_h(j + 2)
            evacuate_z(j + 1)
            plain_out(j + 1, 0)
            plain_out(j + 1, 1)
            if j + 1 == LAST:
                quantize(j + 1)
            add_mx(j, 0)
            add_mx(j, 1)
            gate(j, 0)
            gate(j, 1)
            if 1 <= j <= LAST_ADDED + 1:
                for a in range(2):
                    accumulate(j - 1, nc.gpsimd, slice(0, g_cols(j)), slice(a, a + 1))
            if j == STEPS_PER_HALF + 1:
                nc.gpsimd.tensor_tensor(out=o_sb[0], in0=acc[0][:, 0, :], in1=acc[0][:, 1, :], op=ALU.add)
            if j + 1 < LAST:
                quantize(j + 1)
            if 1 <= j <= LAST_ADDED + 1:
                accumulate(j - 1, nc.vector, slice(g_cols(j), CH))
            if j + 1 < LAST:
                times_cells(j, 0)
                times_cells(j, 1)
            if j == STEPS_PER_HALF + 1:
                nc.sync.dma_start(out=out_0[0:P, :], in_=o_sb[0])

        mx_ps[LAST, 0] = bank("ht", 1)
        mx_part(mx_ps[LAST, 0], LAST, 0, 0, CH)
        halves = [slice(c * HALF, (c + 1) * HALF) for c in range(2)]
        last_ps = []
        for c in range(2):
            last_ps.append(bank("zt", 2))
            mx_part(last_ps[c], LAST, 1, c * HALF, (c + 1) * HALF)
        prod = product_tile(LAST)

        o_t = [bank("pl", 2), bank("pl", 2)]

        def add_turned(src, c, first=False, last=False):
            for i in range(2):
                nc.tensor.matmul(
                    out=o_t[c][:, i * P : (i + 1) * P],
                    lhsT=src[:, (2 * c + i) * P : (2 * c + i + 1) * P],
                    rhs=ident[:],
                    is_transpose=True,
                    start=(first and i == 0),
                    stop=(last and i == 1),
                )

        add_mx(LAST, 0)
        gate(LAST, 0)
        for c in range(2):
            nc.vector.tensor_tensor(out=gates[LAST][:, 1, halves[c]], in0=last_ps[c][:, 0:HALF], in1=tmp[LAST, 1][:, halves[c]], op=ALU.add)
            nc.scalar.activation(out=gates[LAST][:, 1, halves[c]], in_=gates[LAST][:, 1, halves[c]], func=ACT.Sigmoid)
        times_cells(LAST - 1, 0)
        times_cells(LAST - 1, 1)
        for a in range(2):
            for c in range(2):
                add_turned(acc[1][:, a, :], c, first=(a == 0))
        for j in range(LAST_ADDED + 1, LAST):
            for a in range(2):
                for c in range(2):
                    add_turned(p_sb[j][:, a, :], c)
        nc.vector.tensor_tensor(out=prod[:, 0, :], in0=gates[LAST][:, 0, :], in1=cells(LAST)[:, 0, :], op=ALU.mult)
        for c in range(2):
            add_turned(prod[:, 0, :], c)
        ot_sb = keep.tile([P, CH], F32, name="ot_sb")
        back = bank("mx", 2)
        for c in range(2):
            nc.vector.tensor_tensor(out=prod[:, 1, halves[c]], in0=gates[LAST][:, 1, halves[c]], in1=cells(LAST)[:, 1, halves[c]], op=ALU.mult)
            add_turned(prod[:, 1, :], c, last=True)
        reduce_part(0, o_sb[0])
        spread_part(0)
        junk = keep.tile([P, 3 * P], F32, name="junk")
        scale0 = keep.tile([P, 1], F32, name="scale0")
        for c in range(2):
            nc.scalar.copy(out=ot_sb[:, halves[c]], in_=o_t[c][:, 0:HALF])
            reduce_part(1 + c, ot_sb[:, halves[c]])
            for i in range(2):
                blk = slice((2 * c + i) * P, (2 * c + i + 1) * P)
                nc.tensor.transpose(out=back[:, blk], in_=ot_sb[:, blk], identity=ident[:])
            spread_part(1 + c)
        nc.vector.tensor_scalar(
            out=junk[:, 0:P], in0=spread[:, 0:P], scalar1=1.0 / 448.0, scalar2=None, op0=ALU.mult, op1=ALU.max, accum_out=scale0[:, 0:1]
        )
        nc.scalar.copy(out=o_sb[1], in_=back[:])
        nc.sync.dma_start(out=out_0[P : 2 * P, :], in_=o_sb[1])

        scale = keep.tile([P, 1], F32, name="scale")
        nc.vector.tensor_scalar(
            out=junk[:, P : 3 * P], in0=spread[:, P : 3 * P], scalar1=1.0 / 448.0, scalar2=scale0[:, 0:1], op0=ALU.mult, op1=ALU.max,
            accum_out=scale[:, 0:1],
        )
        factor = keep.tile([P, 1], F32, name="factor")
        nc.vector.reciprocal(out=factor[:], in_=scale[:])
        o8 = keep.tile([P, 2, CH], FP8, name="o8")
        o_flat = o_all[:].rearrange("p h c -> p (h c)")
        o8_flat = o8[:].rearrange("p h c -> p (h c)")
        nc.vector.tensor_scalar(
            out=o8_flat[:, S_CAST:], in0=o_flat[:, S_CAST:], scalar1=factor[:, 0:1], scalar2=None, op0=ALU.mult, saturate=False
        )
        nc.scalar.activation(
            out=o8_flat[:, 0:S_CAST], in_=o_flat[:, 0:S_CAST], func=ACT.Identity, scale=factor[:, 0:1], bias=zcol[:, 0:1], saturate=False
        )
        nc.sync.dma_start(out=out_1.rearrange("(h p) c -> p h c", p=P), in_=o8[:].bitcast(U8))
